import numpy as np
import ml_dtypes


def mxq(x, axis, fmt="e4m3"):
    dtype, down = {"e4m3": (ml_dtypes.float8_e4m3fn, 7), "e5m2": (ml_dtypes.float8_e5m2, 14)}[fmt]
    v = np.moveaxis(np.asarray(x, np.float32).astype(ml_dtypes.bfloat16).astype(np.float64), axis, -1)
    blocks = v.reshape(v.shape[:-1] + (-1, 32))
    amax = np.abs(blocks).max(-1, keepdims=True)
    byte = np.maximum(np.where(amax > 0, np.frexp(amax)[1] - 1 + 127, 0) - down, 1)
    scale = np.exp2(byte - 127.0)
    codes = (blocks / scale).astype(np.float32).astype(dtype).astype(np.float64)
    return np.moveaxis((codes * scale).reshape(v.shape), -1, axis)


WIDE = False


def mx_kscale(k):
    if not WIDE:
        return np.ones(k)
    levels = np.array([10, -10, 5, -5, 0])
    a = np.random.permutation(np.resize(levels, k // 512 * 4)).reshape(k // 512, 4)
    idx = np.arange(k)
    return np.exp2(a[idx // 512, idx % 128 // 32])


BF16 = ml_dtypes.bfloat16


def bf(x):
    return np.asarray(x, np.float32).astype(BF16)


def f64(x):
    return np.asarray(x).astype(np.float64)


E2M1 = np.array([0.0, 0.5, 1.0, 1.5, 2.0, 3.0, 4.0, 6.0, -0.0, -0.5, -1.0, -1.5, -2.0, -3.0, -4.0, -6.0])


def pack_weight(w, fmt):
    k, n = w.shape
    w = f64(bf(w)).reshape(k // 32, 32, n)
    amax = np.abs(w).max(1)
    if fmt == "e4m3":
        byte = np.frexp(amax)[1] - 1 + 127 - 7
    else:
        mant, ex = np.frexp(amax / 6.0)
        byte = np.where(mant > 0.5, ex, ex - 1) + 127
    byte = np.clip(np.where(amax > 0, byte, 1), 1, 254)
    scaled = (w * np.exp2(127.0 - byte)[:, None, :]).reshape(k, n).astype(np.float32)
    by_word = np.ascontiguousarray(scaled.reshape(k // 512, 128, 4, n).transpose(0, 1, 3, 2))
    if fmt == "e4m3":
        words = by_word.astype(ml_dtypes.float8_e4m3fn).view(np.uint8)
    else:
        c = by_word.astype(ml_dtypes.float4_e2m1fn).view(np.uint8) & 0xF
        words = c[..., 0::2] | (c[..., 1::2] << 4)
    return np.ascontiguousarray(words), np.ascontiguousarray(byte.astype(np.uint8).reshape(k // 512, 16, n))


def unpack_weight(words, scales, fmt):
    g, p, n, _ = words.shape
    if fmt == "e4m3":
        vals = np.ascontiguousarray(words).view(ml_dtypes.float8_e4m3fn).astype(np.float64)
    else:
        nib = np.empty((g, p, n, 4), np.uint8)
        nib[..., 0::2] = words & 0xF
        nib[..., 1::2] = words >> 4
        vals = E2M1[nib]
    vals = vals * np.repeat(np.exp2(scales.astype(np.float64) - 127.0), 8, axis=1)[..., None]
    return vals.transpose(0, 1, 3, 2).reshape(g * 512, n)


BATCH, IN_F, OUT_F = 128, 8192, 4096
Q_IN = IN_F // 4
Q_OUT = OUT_F // 4
FMT = "e4m3"


def setup_inputs():
    sq = mx_kscale(IN_F)[:Q_IN]
    s = np.tile(sq, 4)
    c = 1.0 / np.sqrt(Q_IN)
    x = bf(np.random.standard_normal((BATCH, IN_F)) * s)
    Wr_words, Wr_scales = pack_weight((np.random.standard_normal((Q_OUT, Q_IN)) * c / sq).T, FMT)
    Wi_words, Wi_scales = pack_weight((np.random.standard_normal((Q_OUT, Q_IN)) * c / sq).T, FMT)
    Wj_words, Wj_scales = pack_weight((np.random.standard_normal((Q_OUT, Q_IN)) * c / sq).T, FMT)
    Wk_words, Wk_scales = pack_weight((np.random.standard_normal((Q_OUT, Q_IN)) * c / sq).T, FMT)
    b = bf(np.random.standard_normal(Q_OUT) * 0.5)
    return {
        "x": x,
        "Wr_words": Wr_words,
        "Wr_scales": Wr_scales,
        "Wi_words": Wi_words,
        "Wi_scales": Wi_scales,
        "Wj_words": Wj_words,
        "Wj_scales": Wj_scales,
        "Wk_words": Wk_words,
        "Wk_scales": Wk_scales,
        "b": b,
    }


def _qdense(x, Wr_t, Wi_t, Wj_t, Wk_t, b):
    W_block = np.concatenate([
        np.concatenate([Wr_t, Wi_t, Wj_t, Wk_t], axis=1),
        np.concatenate([-Wi_t, Wr_t, -Wk_t, Wj_t], axis=1),
        np.concatenate([-Wj_t, Wk_t, Wr_t, -Wi_t], axis=1),
        np.concatenate([-Wk_t, -Wj_t, Wi_t, Wr_t], axis=1),
    ], axis=0)
    b_full = np.concatenate([b, b, b, b])
    return (mxq(x, 1, "e4m3") @ W_block) + b_full


def reference(x, Wr_words, Wr_scales, Wi_words, Wi_scales, Wj_words, Wj_scales, Wk_words, Wk_scales, b):
    return _qdense(
        f64(x),
        unpack_weight(Wr_words, Wr_scales, FMT),
        unpack_weight(Wi_words, Wi_scales, FMT),
        unpack_weight(Wj_words, Wj_scales, FMT),
        unpack_weight(Wk_words, Wk_scales, FMT),
        f64(b),
    )

@@ -1,0 +1,162 @@
+from contextlib import ExitStack
+
+from concourse import mybir
+from concourse.masks import make_identity
+
+F32 = mybir.dt.float32
+BF16 = mybir.dt.bfloat16
+I32 = mybir.dt.int32
+U32 = mybir.dt.uint32
+U8 = mybir.dt.uint8
+FP8X4 = mybir.dt.float8_e4m3fn_x4
+ADD = mybir.AluOpType.add
+MULT = mybir.AluOpType.mult
+
+P = 128
+QUARTERS = 4
+GROUPS = 4
+Q_IN = 2048
+Q_OUT = 1024
+N_TILE = 512
+HALVES = Q_OUT // N_TILE
+
+FLOPS = 2 * 128 * 8192 * 4096
+
+SOURCE = (
+    ((0, 1), (1, 1), (2, 1), (3, 1)),
+    ((1, -1), (0, 1), (3, 1), (2, -1)),
+    ((2, -1), (3, -1), (0, 1), (1, 1)),
+    ((3, -1), (2, 1), (1, -1), (0, 1)),
+)
+
+
+def tile_qdense_w_kernel(
+    tc, x, Wr_words, Wr_scales, Wi_words, Wi_scales, Wj_words, Wj_scales, Wk_words, Wk_scales, b, out
+):
+    nc = tc.nc
+    words_in = (Wr_words, Wi_words, Wj_words, Wk_words)
+    scales_in = (Wr_scales, Wi_scales, Wj_scales, Wk_scales)
+
+    with ExitStack() as ctx:
+        keep = ctx.enter_context(tc.tile_pool(name="keep", bufs=1))
+        psum = ctx.enter_context(tc.psum_pool(name="psum", bufs=1))
+        ctx.enter_context(tc.manual_schedule())
+
+        ident = keep.tile([P, P], F32, name="ident")
+        make_identity(nc, ident[:])
+
+        planes = [keep.tile([P, Q_OUT], U8, name="planes%d" % w, align_bytes=64) for w in range(4)]
+        for w in range(4):
+            nc.vector.memset(planes[w][:].bitcast(I32), 0)
+
+        x_sb = [keep.tile([P, Q_IN], BF16, name="x%d" % q, align_bytes=64) for q in range(QUARTERS)]
+        w_sb = [
+            [keep.tile([P, 4 * Q_OUT], U8, name="w%dg%d" % (w, g), align_bytes=64) for g in range(GROUPS)]
+            for w in range(4)
+        ]
+        bias = keep.tile([P, Q_OUT], BF16, name="bias")
+
+        def load_x(q):
+            nc.sync.dma_start(out=x_sb[q][:], in_=x[:, Q_IN * q : Q_IN * (q + 1)])
+
+        def load_scales(w):
+            for quad in range(4):
+                nc.sync.dma_start(
+                    out=planes[w][32 * quad : 32 * quad + 16, :].bitcast(I32),
+                    in_=scales_in[w][:, 4 * quad : 4 * quad + 4, :].bitcast(I32),
+                )
+
+        def load_words(w):
+            for g in range(GROUPS):
+                nc.sync.dma_start(
+                    out=w_sb[w][g][:].bitcast(I32),
+                    in_=words_in[w][g].rearrange("p n t -> p (n t)").bitcast(I32),
+                )
+
+        load_x(0)
+        load_scales(0)
+        load_x(1)
+        load_x(2)
+        load_x(3)
+        load_words(0)
+        for w in range(1, 4):
+            load_scales(w)
+            load_words(w)
+        nc.sync.dma_start(out=bias[:], in_=b.partition_broadcast(P))
+
+        grouped = [keep.tile([P, Q_IN], BF16, name="grp%d" % q, align_bytes=64) for q in range(QUARTERS)]
+        codes = {}
+        xplanes = {}
+        for q in range(QUARTERS):
+            for sign in (1, -1):
+                if q == 0 and sign == -1:
+                    continue
+                codes[(q, sign)] = keep.tile([P, Q_IN // 4], U32, name="xc%d_%d" % (q, sign + 1), align_bytes=64)
+                xplanes[(q, sign)] = keep.tile([P, Q_IN // 4], U8, name="xs%d_%d" % (q, sign + 1), align_bytes=64)
+
+        def quantise_half(q, j):
+            nc.vector.quantize_mx(
+                out=codes[(q, 1)][:, 256 * j : 256 * (j + 1)].bitcast(FP8X4),
+                scales=xplanes[(q, 1)][:, 256 * j : 256 * (j + 1)],
+                in_=grouped[q][:, 1024 * j : 1024 * (j + 1)],
+            )
+
+        for q in range(QUARTERS):
+            x_words = x_sb[q][:].bitcast(F32)
+            grouped_words = grouped[q][:].bitcast(F32).rearrange("p (g m u) -> p g m u", g=GROUPS, u=2)
+            for j in range(2):
+                xt = psum.tile([P, 2, 2, P], F32, name="xt%d" % (2 * q + j), tag="bank%d" % (2 * q + j))
+                for gg in range(2):
+                    g = 2 * j + gg
+                    for u in range(2):
+                        nc.tensor.transpose(xt[:, gg, u, :], x_words[:, 256 * g + u : 256 * (g + 1) : 2], ident[:])
+                dst = grouped_words[:, 2 * j : 2 * j + 2]
+                src = xt[:].rearrange("p g u m -> p g m u")
+                if j == 0:
+                    nc.vector.tensor_copy(out=dst, in_=src)
+                    if q > 0:
+                        quantise_half(q - 1, 1)
+                    quantise_half(q, 0)
+                else:
+                    nc.scalar.copy(out=dst, in_=src)
+        quantise_half(QUARTERS - 1, 1)
+
+        for q in range(1, QUARTERS):
+            negated = keep.tile([P, Q_IN], BF16, name="neg%d" % q, align_bytes=64)
+            nc.vector.tensor_scalar(out=negated[:], in0=grouped[q][:], scalar1=-1.0, scalar2=None, op0=MULT)
+            nc.vector.quantize_mx(
+                out=codes[(q, -1)][:].bitcast(FP8X4), scales=xplanes[(q, -1)][:], in_=negated[:]
+            )
+
+        acc = [psum.tile([P, N_TILE], F32, name="acc%d" % bank, tag="bank%d" % bank) for bank in range(8)]
+
+        def mx_pass(w, g, c, h):
+            key = SOURCE[w][c]
+            m_cols = slice(P * g, P * (g + 1))
+            n_cols = slice(N_TILE * h, N_TILE * (h + 1))
+            nc.tensor.matmul_mx(
+                out=acc[2 * c + h][:],
+                lhsT=codes[key][:, m_cols].bitcast(FP8X4),
+                lhsT_scale=xplanes[key][:, m_cols],
+                rhs=w_sb[w][g][:, 4 * N_TILE * h : 4 * N_TILE * (h + 1)].bitcast(FP8X4),
+                rhs_scale=planes[w][4 * g : P, n_cols],
+                start=(w == 0 and g == 0),
+                stop=(w == 3 and g == GROUPS - 1),
+            )
+
+        for w in range(3):
+            for g in range(GROUPS):
+                for c in range(4):
+                    for h in range(HALVES):
+                        mx_pass(w, g, c, h)
+        for c in range(4):
+            for h in range(HALVES):
+                for g in range(GROUPS):
+                    mx_pass(3, g, c, h)
+                result = keep.tile([P, N_TILE], F32, name="res%d" % (2 * c + h))
+                nc.vector.tensor_tensor(
+                    out=result[:], in0=acc[2 * c + h][:], in1=bias[:, N_TILE * h : N_TILE * (h + 1)], op=ADD
+                )
+                nc.sync.dma_start(
+                    out=out[:, Q_OUT * c + N_TILE * h : Q_OUT * c + N_TILE * (h + 1)], in_=result[:]
+                )

@@ -66,22 +66,25 @@ def tile_qdense_w_kernel(
                     in_=scales_in[w][:, 4 * quad : 4 * quad + 4, :].bitcast(I32),
                 )
 
-        def load_words(w):
-            for g in range(GROUPS):
-                nc.sync.dma_start(
-                    out=w_sb[w][g][:].bitcast(I32),
-                    in_=words_in[w][g].rearrange("p n t -> p (n t)").bitcast(I32),
-                )
+        def load_words(w, g, pieces=1):
+            width = 4 * Q_OUT // pieces
+            source = words_in[w][g].rearrange("p n t -> p (n t)")
+            for piece in range(pieces):
+                cols = slice(width * piece, width * (piece + 1))
+                nc.sync.dma_start(out=w_sb[w][g][:, cols].bitcast(I32), in_=source[:, cols].bitcast(I32))
 
         load_x(0)
         load_scales(0)
         load_x(1)
         load_x(2)
+        load_words(0, 0, pieces=2)
         load_x(3)
-        load_words(0)
+        for g in range(1, GROUPS):
+            load_words(0, g)
         for w in range(1, 4):
             load_scales(w)
-            load_words(w)
+            for g in range(GROUPS):
+                load_words(w, g)
         nc.sync.dma_start(out=bias[:], in_=b.partition_broadcast(P))
 
         grouped = [keep.tile([P, Q_IN], BF16, name="grp%d" % q, align_bytes=64) for q in range(QUARTERS)]
@@ -101,7 +104,14 @@ def tile_qdense_w_kernel(
                 in_=grouped[q][:, 1024 * j : 1024 * (j + 1)],
             )
 
-        for q in range(QUARTERS):
+        def negate_and_quantise(q):
+            negated = keep.tile([P, Q_IN], BF16, name="neg%d" % q, align_bytes=64)
+            nc.vector.tensor_scalar(out=negated[:], in0=grouped[q][:], scalar1=-1.0, scalar2=None, op0=MULT)
+            nc.vector.quantize_mx(
+                out=codes[(q, -1)][:].bitcast(FP8X4), scales=xplanes[(q, -1)][:], in_=negated[:]
+            )
+
+        def transpose_quarter(q):
             x_words = x_sb[q][:].bitcast(F32)
             grouped_words = grouped[q][:].bitcast(F32).rearrange("p (g m u) -> p g m u", g=GROUPS, u=2)
             for j in range(2):
@@ -114,49 +124,77 @@ def tile_qdense_w_kernel(
                 src = xt[:].rearrange("p g u m -> p g m u")
                 if j == 0:
                     nc.vector.tensor_copy(out=dst, in_=src)
-                    if q > 0:
-                        quantise_half(q - 1, 1)
-                    quantise_half(q, 0)
                 else:
                     nc.scalar.copy(out=dst, in_=src)
-        quantise_half(QUARTERS - 1, 1)
 
-        for q in range(1, QUARTERS):
-            negated = keep.tile([P, Q_IN], BF16, name="neg%d" % q, align_bytes=64)
-            nc.vector.tensor_scalar(out=negated[:], in0=grouped[q][:], scalar1=-1.0, scalar2=None, op0=MULT)
-            nc.vector.quantize_mx(
-                out=codes[(q, -1)][:].bitcast(FP8X4), scales=xplanes[(q, -1)][:], in_=negated[:]
-            )
+        acc = {}
 
-        acc = [psum.tile([P, N_TILE], F32, name="acc%d" % bank, tag="bank%d" % bank) for bank in range(8)]
-
-        def mx_pass(w, g, c, h):
+        def mx_pass(w, g, c, n0, width, bank, start, stop):
             key = SOURCE[w][c]
             m_cols = slice(P * g, P * (g + 1))
-            n_cols = slice(N_TILE * h, N_TILE * (h + 1))
             nc.tensor.matmul_mx(
-                out=acc[2 * c + h][:],
+                out=acc[bank][:],
                 lhsT=codes[key][:, m_cols].bitcast(FP8X4),
                 lhsT_scale=xplanes[key][:, m_cols],
-                rhs=w_sb[w][g][:, 4 * N_TILE * h : 4 * N_TILE * (h + 1)].bitcast(FP8X4),
-                rhs_scale=planes[w][4 * g : P, n_cols],
-                start=(w == 0 and g == 0),
-                stop=(w == 3 and g == GROUPS - 1),
+                rhs=w_sb[w][g][:, 4 * n0 : 4 * (n0 + width)].bitcast(FP8X4),
+                rhs_scale=planes[w][4 * g : P, n0 : n0 + width],
+                start=start,
+                stop=stop,
             )
 
-        for w in range(3):
-            for g in range(GROUPS):
-                for c in range(4):
-                    for h in range(HALVES):
-                        mx_pass(w, g, c, h)
-        for c in range(4):
+        def wide_pass(w, g, c, h):
+            bank = 2 * c + h
+            if w == 0 and g == 0:
+                acc[bank] = psum.tile([P, N_TILE], F32, name="acc%d" % bank, tag="bank%d" % bank)
+            mx_pass(w, g, c, N_TILE * h, N_TILE, bank, w == 0 and g == 0, w == 3 and g == GROUPS - 1)
+
+        def finish(bank, c, n0, width):
+            result = keep.tile([P, width], F32, name="res%s" % bank)
+            nc.vector.tensor_tensor(out=result[:], in0=acc[bank][:], in1=bias[:, n0 : n0 + width], op=ADD)
+            nc.sync.dma_start(out=out[:, Q_OUT * c + n0 : Q_OUT * c + n0 + width], in_=result[:])
+
+        LATE = (3, 1)
+        early = [(c, h) for c in range(4) for h in range(HALVES) if (c, h) != LATE]
+
+        transpose_quarter(0)
+        quantise_half(0, 0)
+        transpose_quarter(1)
+        quantise_half(0, 1)
+        quantise_half(1, 0)
+        transpose_quarter(2)
+        quantise_half(1, 1)
+        quantise_half(2, 0)
+        quantise_half(2, 1)
+        negate_and_quantise(1)
+        for h in range(HALVES):
+            for c in range(3):
+                wide_pass(0, 0, c, h)
+        transpose_quarter(3)
+        quantise_half(3, 0)
+        quantise_half(3, 1)
+        negate_and_quantise(2)
+        negate_and_quantise(3)
+        for c in range(3):
             for h in range(HALVES):
+                wide_pass(0, 1, c, h)
+        wide_pass(0, 0, 3, 0)
+        wide_pass(0, 1, 3, 0)
+        for g in range(2, GROUPS):
+            for c, h in early:
+                wide_pass(0, g, c, h)
+        for w in range(1, 3):
+            for g in range(GROUPS):
+                for c, h in early:
+                    wide_pass(w, g, c, h)
+        for c, h in early:
+            for g in range(GROUPS):
+                wide_pass(3, g, c, h)
+            finish(2 * c + h, c, N_TILE * h, N_TILE)
+        for s in range(2):
+            name = "late%d" % s
+            acc[name] = psum.tile([P, N_TILE // 2], F32, name=name, tag="bank%d" % (7 * (1 - s)))
+            n0 = N_TILE * LATE[1] + (N_TILE // 2) * s
+            for w in range(4):
                 for g in range(GROUPS):
-                    mx_pass(3, g, c, h)
-                result = keep.tile([P, N_TILE], F32, name="res%d" % (2 * c + h))
-                nc.vector.tensor_tensor(
-                    out=result[:], in0=acc[2 * c + h][:], in1=bias[:, N_TILE * h : N_TILE * (h + 1)], op=ADD
-                )
-                nc.sync.dma_start(
-                    out=out[:, Q_OUT * c + N_TILE * h : Q_OUT * c + N_TILE * (h + 1)], in_=result[:]
-                )
+                    mx_pass(w, g, LATE[0], n0, N_TILE // 2, name, w == 0 and g == 0, w == 3 and g == GROUPS - 1)
+            finish(name, LATE[0], n0, N_TILE // 2)

@@ -19,6 +19,7 @@ Q_IN = 2048
 Q_OUT = 1024
 N_TILE = 512
 HALVES = Q_OUT // N_TILE
+SHIFT = 48
 
 FLOPS = 2 * 128 * 8192 * 4096
 
@@ -45,13 +46,13 @@ def tile_qdense_w_kernel(
         ident = keep.tile([P, P], F32, name="ident")
         make_identity(nc, ident[:])
 
-        planes = [keep.tile([P, Q_OUT], U8, name="planes%d" % w, align_bytes=64) for w in range(4)]
+        planes = [keep.tile([P, Q_OUT], U8, name="planes%d" % w, align_bytes=256) for w in range(4)]
         for w in range(4):
             nc.vector.memset(planes[w][:].bitcast(I32), 0)
 
         x_sb = [keep.tile([P, Q_IN], BF16, name="x%d" % q, align_bytes=64) for q in range(QUARTERS)]
         w_sb = [
-            [keep.tile([P, 4 * Q_OUT], U8, name="w%dg%d" % (w, g), align_bytes=64) for g in range(GROUPS)]
+            [keep.tile([P, 4 * Q_OUT], U8, name="w%dg%d" % (w, g), align_bytes=256) for g in range(GROUPS)]
             for w in range(4)
         ]
         bias = keep.tile([P, Q_OUT], BF16, name="bias")
@@ -94,22 +95,27 @@ def tile_qdense_w_kernel(
             for sign in (1, -1):
                 if q == 0 and sign == -1:
                     continue
-                codes[(q, sign)] = keep.tile([P, Q_IN // 4], U32, name="xc%d_%d" % (q, sign + 1), align_bytes=64)
-                xplanes[(q, sign)] = keep.tile([P, Q_IN // 4], U8, name="xs%d_%d" % (q, sign + 1), align_bytes=64)
+                codes[(q, sign)] = keep.tile(
+                    [P, SHIFT + Q_IN // 4], U32, name="xc%d_%d" % (q, sign + 1), align_bytes=256
+                )
+                xplanes[(q, sign)] = keep.tile([P, GROUPS, 256], U8, name="xs%d_%d" % (q, sign + 1), align_bytes=256)
+
+        def quantise_group(key, g, values):
+            nc.vector.quantize_mx(
+                out=codes[key][:, SHIFT + P * g : SHIFT + P * (g + 1)].bitcast(FP8X4),
+                scales=xplanes[key][:, g, 0:P],
+                in_=values[:, 4 * P * g : 4 * P * (g + 1)],
+            )
 
         def quantise_half(q, j):
-            nc.vector.quantize_mx(
-                out=codes[(q, 1)][:, 256 * j : 256 * (j + 1)].bitcast(FP8X4),
-                scales=xplanes[(q, 1)][:, 256 * j : 256 * (j + 1)],
-                in_=grouped[q][:, 1024 * j : 1024 * (j + 1)],
-            )
+            for g in (2 * j, 2 * j + 1):
+                quantise_group((q, 1), g, grouped[q])
 
         def negate_and_quantise(q):
             negated = keep.tile([P, Q_IN], BF16, name="neg%d" % q, align_bytes=64)
             nc.vector.tensor_scalar(out=negated[:], in0=grouped[q][:], scalar1=-1.0, scalar2=None, op0=MULT)
-            nc.vector.quantize_mx(
-                out=codes[(q, -1)][:].bitcast(FP8X4), scales=xplanes[(q, -1)][:], in_=negated[:]
-            )
+            for g in range(GROUPS):
+                quantise_group((q, -1), g, negated)
 
         def transpose_quarter(q):
             x_words = x_sb[q][:].bitcast(F32)
@@ -131,11 +137,10 @@ def tile_qdense_w_kernel(
 
         def mx_pass(w, g, c, n0, width, bank, start, stop):
             key = SOURCE[w][c]
-            m_cols = slice(P * g, P * (g + 1))
             nc.tensor.matmul_mx(
                 out=acc[bank][:],
-                lhsT=codes[key][:, m_cols].bitcast(FP8X4),
-                lhsT_scale=xplanes[key][:, m_cols],
+                lhsT=codes[key][:, SHIFT + P * g : SHIFT + P * (g + 1)].bitcast(FP8X4),
+                lhsT_scale=xplanes[key][:, g, 0:P],
                 rhs=w_sb[w][g][:, 4 * n0 : 4 * (n0 + width)].bitcast(FP8X4),
                 rhs_scale=planes[w][4 * g : P, n0 : n0 + width],
                 start=start,

@@ -15,6 +15,7 @@ MULT = mybir.AluOpType.mult
 P = 128
 QUARTERS = 4
 GROUPS = 4
+K_PASS = 512
 Q_IN = 2048
 Q_OUT = 1024
 N_TILE = 512
@@ -50,15 +51,20 @@ def tile_qdense_w_kernel(
         for w in range(4):
             nc.vector.memset(planes[w][:].bitcast(I32), 0)
 
-        x_sb = [keep.tile([P, Q_IN], BF16, name="x%d" % q, align_bytes=64) for q in range(QUARTERS)]
+        x_sb = [keep.tile([P, QUARTERS * K_PASS], BF16, name="x%d" % g, align_bytes=64) for g in range(GROUPS)]
         w_sb = [
             [keep.tile([P, 4 * Q_OUT], U8, name="w%dg%d" % (w, g), align_bytes=256) for g in range(GROUPS)]
             for w in range(4)
         ]
         bias = keep.tile([P, Q_OUT], BF16, name="bias")
+        x_by_group = x.rearrange("m (q g k) -> m q g k", q=QUARTERS, g=GROUPS)
 
-        def load_x(q):
-            nc.sync.dma_start(out=x_sb[q][:], in_=x[:, Q_IN * q : Q_IN * (q + 1)])
+        def load_x(g, pieces=1):
+            count = QUARTERS // pieces
+            dst = x_sb[g][:].rearrange("p (q k) -> p q k", q=QUARTERS)
+            for piece in range(pieces):
+                qs = slice(count * piece, count * (piece + 1))
+                nc.sync.dma_start(out=dst[:, qs, :], in_=x_by_group[:, qs, g, :])
 
         def load_scales(w):
             for quad in range(4):
@@ -74,21 +80,28 @@ def tile_qdense_w_kernel(
                 cols = slice(width * piece, width * (piece + 1))
                 nc.sync.dma_start(out=w_sb[w][g][:, cols].bitcast(I32), in_=source[:, cols].bitcast(I32))
 
-        load_x(0)
+        load_x(0, pieces=2)
         load_scales(0)
-        load_x(1)
-        load_x(2)
         load_words(0, 0, pieces=2)
-        load_x(3)
+        load_x(1)
+        load_scales(1)
+        load_words(1, 0)
         for g in range(1, GROUPS):
             load_words(0, g)
-        for w in range(1, 4):
-            load_scales(w)
-            for g in range(GROUPS):
-                load_words(w, g)
+            if g + 1 < GROUPS:
+                load_x(g + 1)
+            load_words(1, g)
+        load_scales(2)
+        load_words(2, 0)
+        load_scales(3)
+        load_words(3, 0)
+        for g in range(1, GROUPS):
+            load_words(2, g)
+            load_words(3, g)
         nc.sync.dma_start(out=bias[:], in_=b.partition_broadcast(P))
 
-        grouped = [keep.tile([P, Q_IN], BF16, name="grp%d" % q, align_bytes=64) for q in range(QUARTERS)]
+        grouped = [keep.tile([P, QUARTERS * K_PASS], BF16, name="grp%d" % g, align_bytes=64) for g in range(GROUPS)]
+        negated = [keep.tile([P, QUARTERS * K_PASS], BF16, name="neg%d" % g, align_bytes=64) for g in range(GROUPS)]
         codes = {}
         xplanes = {}
         for q in range(QUARTERS):
@@ -100,38 +113,42 @@ def tile_qdense_w_kernel(
                 )
                 xplanes[(q, sign)] = keep.tile([P, GROUPS, 256], U8, name="xs%d_%d" % (q, sign + 1), align_bytes=256)
 
-        def quantise_group(key, g, values):
+        def quantise(q, sign, g):
+            values = grouped[g] if sign == 1 else negated[g]
             nc.vector.quantize_mx(
-                out=codes[key][:, SHIFT + P * g : SHIFT + P * (g + 1)].bitcast(FP8X4),
-                scales=xplanes[key][:, g, 0:P],
-                in_=values[:, 4 * P * g : 4 * P * (g + 1)],
+                out=codes[(q, sign)][:, SHIFT + P * g : SHIFT + P * (g + 1)].bitcast(FP8X4),
+                scales=xplanes[(q, sign)][:, g, 0:P],
+                in_=values[:, K_PASS * q : K_PASS * (q + 1)],
             )
 
-        def quantise_half(q, j):
-            for g in (2 * j, 2 * j + 1):
-                quantise_group((q, 1), g, grouped[q])
+        def negate(g, q0, q1):
+            cols = slice(K_PASS * q0, K_PASS * q1)
+            nc.vector.tensor_scalar(
+                out=negated[g][:, cols], in0=grouped[g][:, cols], scalar1=-1.0, scalar2=None, op0=MULT
+            )
 
-        def negate_and_quantise(q):
-            negated = keep.tile([P, Q_IN], BF16, name="neg%d" % q, align_bytes=64)
-            nc.vector.tensor_scalar(out=negated[:], in0=grouped[q][:], scalar1=-1.0, scalar2=None, op0=MULT)
-            for g in range(GROUPS):
-                quantise_group((q, -1), g, negated)
-
-        def transpose_quarter(q):
-            x_words = x_sb[q][:].bitcast(F32)
-            grouped_words = grouped[q][:].bitcast(F32).rearrange("p (g m u) -> p g m u", g=GROUPS, u=2)
-            for j in range(2):
-                xt = psum.tile([P, 2, 2, P], F32, name="xt%d" % (2 * q + j), tag="bank%d" % (2 * q + j))
-                for gg in range(2):
-                    g = 2 * j + gg
+        def prepare_group(g):
+            x_words = x_sb[g][:].bitcast(F32)
+            grouped_words = grouped[g][:].bitcast(F32).rearrange("p (q m u) -> p q m u", q=QUARTERS, u=2)
+            banks = []
+            for pair in range(2):
+                xt = psum.tile([P, 2, 2, P], F32, name="xt%d_%d" % (g, pair), tag="bank%d" % (6 + pair))
+                banks.append(xt)
+                for qq in range(2):
+                    q = 2 * pair + qq
                     for u in range(2):
-                        nc.tensor.transpose(xt[:, gg, u, :], x_words[:, 256 * g + u : 256 * (g + 1) : 2], ident[:])
-                dst = grouped_words[:, 2 * j : 2 * j + 2]
-                src = xt[:].rearrange("p g u m -> p g m u")
-                if j == 0:
-                    nc.vector.tensor_copy(out=dst, in_=src)
-                else:
-                    nc.scalar.copy(out=dst, in_=src)
+                        nc.tensor.transpose(xt[:, qq, u, :], x_words[:, 256 * q + u : 256 * (q + 1) : 2], ident[:])
+            nc.scalar.copy(out=grouped_words[:, 0:2], in_=banks[0][:].rearrange("p q u m -> p q m u"))
+            quantise(0, 1, g)
+            quantise(1, 1, g)
+            nc.vector.tensor_copy(out=grouped_words[:, 2:4], in_=banks[1][:].rearrange("p q u m -> p q m u"))
+            negate(g, 1, 2)
+            quantise(2, 1, g)
+            quantise(3, 1, g)
+            negate(g, 2, 4)
+            quantise(1, -1, g)
+            quantise(2, -1, g)
+            quantise(3, -1, g)
 
         acc = {}
 
@@ -147,59 +164,34 @@ def tile_qdense_w_kernel(
                 stop=stop,
             )
 
-        def wide_pass(w, g, c, h):
-            bank = 2 * c + h
-            if w == 0 and g == 0:
-                acc[bank] = psum.tile([P, N_TILE], F32, name="acc%d" % bank, tag="bank%d" % bank)
-            mx_pass(w, g, c, N_TILE * h, N_TILE, bank, w == 0 and g == 0, w == 3 and g == GROUPS - 1)
+        def chunk(w, g):
+            for c in range(3):
+                for h in range(HALVES):
+                    bank = 2 * c + h
+                    if w == 0 and g == 0:
+                        acc[bank] = psum.tile([P, N_TILE], F32, name="acc%d" % bank, tag="bank%d" % bank)
+                    mx_pass(w, g, c, N_TILE * h, N_TILE, bank, w == 0 and g == 0, w == 3 and g == GROUPS - 1)
 
         def finish(bank, c, n0, width):
             result = keep.tile([P, width], F32, name="res%s" % bank)
             nc.vector.tensor_tensor(out=result[:], in0=acc[bank][:], in1=bias[:, n0 : n0 + width], op=ADD)
             nc.sync.dma_start(out=out[:, Q_OUT * c + n0 : Q_OUT * c + n0 + width], in_=result[:])
 
-        LATE = (3, 1)
-        early = [(c, h) for c in range(4) for h in range(HALVES) if (c, h) != LATE]
-
-        transpose_quarter(0)
-        quantise_half(0, 0)
-        transpose_quarter(1)
-        quantise_half(0, 1)
-        quantise_half(1, 0)
-        transpose_quarter(2)
-        quantise_half(1, 1)
-        quantise_half(2, 0)
-        quantise_half(2, 1)
-        negate_and_quantise(1)
-        for h in range(HALVES):
-            for c in range(3):
-                wide_pass(0, 0, c, h)
-        transpose_quarter(3)
-        quantise_half(3, 0)
-        quantise_half(3, 1)
-        negate_and_quantise(2)
-        negate_and_quantise(3)
+        prepare_group(0)
+        for g in range(GROUPS):
+            chunk(0, g)
+            if g + 1 < GROUPS:
+                prepare_group(g + 1)
+            chunk(1, g)
+        for g in range(GROUPS):
+            chunk(2, g)
+            chunk(3, g)
         for c in range(3):
             for h in range(HALVES):
-                wide_pass(0, 1, c, h)
-        wide_pass(0, 0, 3, 0)
-        wide_pass(0, 1, 3, 0)
-        for g in range(2, GROUPS):
-            for c, h in early:
-                wide_pass(0, g, c, h)
-        for w in range(1, 3):
-            for g in range(GROUPS):
-                for c, h in early:
-                    wide_pass(w, g, c, h)
-        for c, h in early:
-            for g in range(GROUPS):
-                wide_pass(3, g, c, h)
-            finish(2 * c + h, c, N_TILE * h, N_TILE)
-        for s in range(2):
-            name = "late%d" % s
-            acc[name] = psum.tile([P, N_TILE // 2], F32, name=name, tag="bank%d" % (7 * (1 - s)))
-            n0 = N_TILE * LATE[1] + (N_TILE // 2) * s
+                finish(2 * c + h, c, N_TILE * h, N_TILE)
+        for name, tag, n0, width in (("late0", 6, 0, 512), ("late1", 7, 512, 256), ("late2", 0, 768, 256)):
+            acc[name] = psum.tile([P, width], F32, name=name, tag="bank%d" % tag)
             for w in range(4):
                 for g in range(GROUPS):
-                    mx_pass(w, g, LATE[0], n0, N_TILE // 2, name, w == 0 and g == 0, w == 3 and g == GROUPS - 1)
-            finish(name, LATE[0], n0, N_TILE // 2)
+                    mx_pass(w, g, 3, n0, width, name, w == 0 and g == 0, w == 3 and g == GROUPS - 1)
+            finish(name, 3, n0, width)

@@ -100,6 +100,9 @@ def tile_qdense_w_kernel(
             load_words(3, g)
         nc.sync.dma_start(out=bias[:], in_=b.partition_broadcast(P))
 
+        ordered = [None, None] + [
+            keep.tile([P, QUARTERS * K_PASS // 2], F32, name="ord%d" % g, align_bytes=64) for g in range(2, GROUPS)
+        ]
         grouped = [keep.tile([P, QUARTERS * K_PASS], BF16, name="grp%d" % g, align_bytes=64) for g in range(GROUPS)]
         negated = [keep.tile([P, QUARTERS * K_PASS], BF16, name="neg%d" % g, align_bytes=64) for g in range(GROUPS)]
         codes = {}
@@ -131,13 +134,22 @@ def tile_qdense_w_kernel(
             x_words = x_sb[g][:].bitcast(F32)
             grouped_words = grouped[g][:].bitcast(F32).rearrange("p (q m u) -> p q m u", q=QUARTERS, u=2)
             banks = []
+            if ordered[g] is not None:
+                nc.scalar.copy(
+                    out=ordered[g][:].rearrange("p (q u i) -> p q u i", q=QUARTERS, u=2),
+                    in_=x_words.rearrange("p (q i u) -> p q u i", q=QUARTERS, u=2),
+                )
             for pair in range(2):
                 xt = psum.tile([P, 2, 2, P], F32, name="xt%d_%d" % (g, pair), tag="bank%d" % (6 + pair))
                 banks.append(xt)
                 for qq in range(2):
                     q = 2 * pair + qq
                     for u in range(2):
-                        nc.tensor.transpose(xt[:, qq, u, :], x_words[:, 256 * q + u : 256 * (q + 1) : 2], ident[:])
+                        if ordered[g] is None:
+                            half = x_words[:, 256 * q + u : 256 * (q + 1) : 2]
+                        else:
+                            half = ordered[g][:, 256 * q + P * u : 256 * q + P * (u + 1)]
+                        nc.tensor.transpose(xt[:, qq, u, :], half, ident[:])
             nc.scalar.copy(out=grouped_words[:, 0:2], in_=banks[0][:].rearrange("p q u m -> p q m u"))
             quantise(0, 1, g)
             quantise(1, 1, g)

@@ -51,13 +51,24 @@ def tile_qdense_w_kernel(
         for w in range(4):
             nc.vector.memset(planes[w][:].bitcast(I32), 0)
 
-        x_sb = [keep.tile([P, QUARTERS * K_PASS], BF16, name="x%d" % g, align_bytes=64) for g in range(GROUPS)]
+        x_first = keep.tile([P, QUARTERS * 2 * K_PASS], BF16, name="x01", align_bytes=64)
+        x_sb = [None, None] + [
+            keep.tile([P, QUARTERS * K_PASS], BF16, name="x%d" % g, align_bytes=64) for g in range(2, GROUPS)
+        ]
         w_sb = [
             [keep.tile([P, 4 * Q_OUT], U8, name="w%dg%d" % (w, g), align_bytes=256) for g in range(GROUPS)]
             for w in range(4)
         ]
         bias = keep.tile([P, Q_OUT], BF16, name="bias")
         x_by_group = x.rearrange("m (q g k) -> m q g k", q=QUARTERS, g=GROUPS)
+
+        def load_first(pieces):
+            count = QUARTERS // pieces
+            dst = x_first[:].rearrange("p (q r) -> p q r", q=QUARTERS)
+            src = x.rearrange("m (q r) -> m q r", q=QUARTERS)
+            for piece in range(pieces):
+                qs = slice(count * piece, count * (piece + 1))
+                nc.sync.dma_start(out=dst[:, qs, :], in_=src[:, qs, 0 : 2 * K_PASS])
 
         def load_x(g, pieces=1):
             count = QUARTERS // pieces
@@ -67,7 +78,7 @@ def tile_qdense_w_kernel(
                 nc.sync.dma_start(out=dst[:, qs, :], in_=x_by_group[:, qs, g, :])
 
         def load_scales(w):
-            for quad in range(4):
+            for quad in (0, 2, 1, 3):
                 nc.sync.dma_start(
                     out=planes[w][32 * quad : 32 * quad + 16, :].bitcast(I32),
                     in_=scales_in[w][:, 4 * quad : 4 * quad + 4, :].bitcast(I32),
@@ -80,23 +91,26 @@ def tile_qdense_w_kernel(
                 cols = slice(width * piece, width * (piece + 1))
                 nc.sync.dma_start(out=w_sb[w][g][:, cols].bitcast(I32), in_=source[:, cols].bitcast(I32))
 
-        load_x(0, pieces=2)
+        load_first(pieces=2)
         load_scales(0)
         load_words(0, 0, pieces=2)
-        load_x(1)
+        load_words(0, 1)
         load_scales(1)
         load_words(1, 0)
-        for g in range(1, GROUPS):
-            load_words(0, g)
-            if g + 1 < GROUPS:
-                load_x(g + 1)
-            load_words(1, g)
+        load_words(1, 1)
+        load_x(2)
         load_scales(2)
         load_words(2, 0)
+        load_words(0, 2)
+        load_words(1, 2)
+        load_x(3)
+        load_words(2, 1)
+        load_words(0, 3)
+        load_words(1, 3)
+        load_words(2, 2)
+        load_words(2, 3)
         load_scales(3)
-        load_words(3, 0)
-        for g in range(1, GROUPS):
-            load_words(2, g)
+        for g in range(GROUPS):
             load_words(3, g)
         nc.sync.dma_start(out=bias[:], in_=b.partition_broadcast(P))
 
@@ -130,25 +144,58 @@ def tile_qdense_w_kernel(
                 out=negated[g][:, cols], in0=grouped[g][:, cols], scalar1=-1.0, scalar2=None, op0=MULT
             )
 
+        def grouped_pair(g, pair):
+            words = grouped[g][:].bitcast(F32).rearrange("p (q m u) -> p q m u", q=QUARTERS, u=2)
+            return words[:, 2 * pair : 2 * pair + 2]
+
+        def prepare_first_two():
+            x_words = x_first[:].bitcast(F32)
+            banks = {}
+            for pair in range(2):
+                for g in range(2):
+                    xt = psum.tile([P, 2, 2, P], F32, name="xt%d_%d" % (g, pair), tag="bank%d" % (6 - 2 * g + pair))
+                    banks[(g, pair)] = xt[:].rearrange("p q u m -> p q m u")
+                    for qq in range(2):
+                        first = 512 * (2 * pair + qq) + 256 * g
+                        for u in range(2):
+                            nc.tensor.transpose(xt[:, qq, u, :], x_words[:, first + u : first + 256 : 2], ident[:])
+            nc.scalar.copy(out=grouped_pair(0, 0), in_=banks[(0, 0)])
+            nc.scalar.copy(out=grouped_pair(1, 0), in_=banks[(1, 0)])
+            quantise(0, 1, 0)
+            quantise(1, 1, 0)
+            nc.vector.tensor_copy(out=grouped_pair(0, 1), in_=banks[(0, 1)])
+            negate(0, 1, 2)
+            quantise(2, 1, 0)
+            quantise(3, 1, 0)
+            nc.vector.tensor_copy(out=grouped_pair(1, 1), in_=banks[(1, 1)])
+            quantise(0, 1, 1)
+            quantise(1, 1, 1)
+            quantise(2, 1, 1)
+            quantise(3, 1, 1)
+            negate(0, 2, 4)
+            quantise(1, -1, 0)
+            quantise(2, -1, 0)
+            quantise(3, -1, 0)
+            negate(1, 1, 4)
+            quantise(1, -1, 1)
+            quantise(2, -1, 1)
+            quantise(3, -1, 1)
+
         def prepare_group(g):
             x_words = x_sb[g][:].bitcast(F32)
             grouped_words = grouped[g][:].bitcast(F32).rearrange("p (q m u) -> p q m u", q=QUARTERS, u=2)
             banks = []
-            if ordered[g] is not None:
-                nc.scalar.copy(
-                    out=ordered[g][:].rearrange("p (q u i) -> p q u i", q=QUARTERS, u=2),
-                    in_=x_words.rearrange("p (q i u) -> p q u i", q=QUARTERS, u=2),
-                )
+            dst = ordered[g][:].rearrange("p (q u i) -> p q u i", q=QUARTERS, u=2)
+            src = x_words.rearrange("p (q i u) -> p q u i", q=QUARTERS, u=2)
+            nc.scalar.copy(out=dst[:, 0:2], in_=src[:, 0:2])
+            nc.vector.tensor_copy(out=dst[:, 2:4], in_=src[:, 2:4])
             for pair in range(2):
                 xt = psum.tile([P, 2, 2, P], F32, name="xt%d_%d" % (g, pair), tag="bank%d" % (6 + pair))
                 banks.append(xt)
                 for qq in range(2):
                     q = 2 * pair + qq
                     for u in range(2):
-                        if ordered[g] is None:
-                            half = x_words[:, 256 * q + u : 256 * (q + 1) : 2]
-                        else:
-                            half = ordered[g][:, 256 * q + P * u : 256 * q + P * (u + 1)]
+                        half = ordered[g][:, 256 * q + P * u : 256 * q + P * (u + 1)]
                         nc.tensor.transpose(xt[:, qq, u, :], half, ident[:])
             nc.scalar.copy(out=grouped_words[:, 0:2], in_=banks[0][:].rearrange("p q u m -> p q m u"))
             quantise(0, 1, g)
@@ -189,14 +236,19 @@ def tile_qdense_w_kernel(
             nc.vector.tensor_tensor(out=result[:], in0=acc[bank][:], in1=bias[:, n0 : n0 + width], op=ADD)
             nc.sync.dma_start(out=out[:, Q_OUT * c + n0 : Q_OUT * c + n0 + width], in_=result[:])
 
-        prepare_group(0)
-        for g in range(GROUPS):
+        prepare_first_two()
+        chunk(0, 0)
+        chunk(0, 1)
+        chunk(1, 0)
+        chunk(1, 1)
+        for g in range(2, GROUPS):
+            prepare_group(g)
+            chunk(2, g - 2)
             chunk(0, g)
-            if g + 1 < GROUPS:
-                prepare_group(g + 1)
             chunk(1, g)
+        chunk(2, 2)
+        chunk(2, 3)
         for g in range(GROUPS):
-            chunk(2, g)
             chunk(3, g)
         for c in range(3):
             for h in range(HALVES):

@@ -44,6 +44,8 @@ def tile_qdense_w_kernel(
         psum = ctx.enter_context(tc.psum_pool(name="psum", bufs=1))
         ctx.enter_context(tc.manual_schedule())
 
+        zeros = keep.tile([P, N_TILE], BF16, name="zeros")
+        nc.vector.memset(zeros[:], 0.0)
         ident = keep.tile([P, P], F32, name="ident")
         make_identity(nc, ident[:])
 
@@ -148,10 +150,19 @@ def tile_qdense_w_kernel(
             words = grouped[g][:].bitcast(F32).rearrange("p (q m u) -> p q m u", q=QUARTERS, u=2)
             return words[:, 2 * pair : 2 * pair + 2]
 
+        warm = psum.tile([P, N_TILE], F32, name="warm", tag="bank3")
+
+        def keep_clock_up(count):
+            for i in range(count):
+                nc.tensor.matmul(out=warm[:], lhsT=zeros[:, 0:P], rhs=zeros[:], start=True, stop=True)
+
         def prepare_first_two():
             x_words = x_first[:].bitcast(F32)
             banks = {}
+            keep_clock_up(6)
             for pair in range(2):
+                if pair == 1:
+                    keep_clock_up(1)
                 for g in range(2):
                     xt = psum.tile([P, 2, 2, P], F32, name="xt%d_%d" % (g, pair), tag="bank%d" % (6 - 2 * g + pair))
                     banks[(g, pair)] = xt[:].rearrange("p q u m -> p q m u")
@@ -159,6 +170,7 @@ def tile_qdense_w_kernel(
                         first = 512 * (2 * pair + qq) + 256 * g
                         for u in range(2):
                             nc.tensor.transpose(xt[:, qq, u, :], x_words[:, first + u : first + 256 : 2], ident[:])
+            keep_clock_up(1)
             nc.scalar.copy(out=grouped_pair(0, 0), in_=banks[(0, 0)])
             nc.scalar.copy(out=grouped_pair(1, 0), in_=banks[(1, 0)])
             quantise(0, 1, 0)

@@ -100,16 +100,16 @@ def tile_qdense_w_kernel(
         load_scales(1)
         load_words(1, 0)
         load_words(1, 1)
-        load_x(2)
         load_scales(2)
         load_words(2, 0)
+        load_x(2)
+        load_words(2, 1)
         load_words(0, 2)
         load_words(1, 2)
         load_x(3)
-        load_words(2, 1)
+        load_words(2, 2)
         load_words(0, 3)
         load_words(1, 3)
-        load_words(2, 2)
         load_words(2, 3)
         load_scales(3)
         for g in range(GROUPS):
@@ -253,12 +253,12 @@ def tile_qdense_w_kernel(
         chunk(0, 1)
         chunk(1, 0)
         chunk(1, 1)
+        chunk(2, 0)
         for g in range(2, GROUPS):
             prepare_group(g)
-            chunk(2, g - 2)
+            chunk(2, g - 1)
             chunk(0, g)
             chunk(1, g)
-        chunk(2, 2)
         chunk(2, 3)
         for g in range(GROUPS):
             chunk(3, g)

from contextlib import ExitStack

from concourse import mybir
from concourse.masks import make_identity

F32 = mybir.dt.float32
BF16 = mybir.dt.bfloat16
I32 = mybir.dt.int32
U32 = mybir.dt.uint32
U8 = mybir.dt.uint8
FP8X4 = mybir.dt.float8_e4m3fn_x4
ADD = mybir.AluOpType.add
MULT = mybir.AluOpType.mult

P = 128
QUARTERS = 4
GROUPS = 4
K_PASS = 512
Q_IN = 2048
Q_OUT = 1024
N_TILE = 512
HALVES = Q_OUT // N_TILE
SHIFT = 48

FLOPS = 2 * 128 * 8192 * 4096

SOURCE = (
    ((0, 1), (1, 1), (2, 1), (3, 1)),
    ((1, -1), (0, 1), (3, 1), (2, -1)),
    ((2, -1), (3, -1), (0, 1), (1, 1)),
    ((3, -1), (2, 1), (1, -1), (0, 1)),
)


def tile_qdense_w_kernel(
    tc, x, Wr_words, Wr_scales, Wi_words, Wi_scales, Wj_words, Wj_scales, Wk_words, Wk_scales, b, out
):
    nc = tc.nc
    words_in = (Wr_words, Wi_words, Wj_words, Wk_words)
    scales_in = (Wr_scales, Wi_scales, Wj_scales, Wk_scales)

    with ExitStack() as ctx:
        keep = ctx.enter_context(tc.tile_pool(name="keep", bufs=1))
        psum = ctx.enter_context(tc.psum_pool(name="psum", bufs=1))
        ctx.enter_context(tc.manual_schedule())

        zeros = keep.tile([P, N_TILE], BF16, name="zeros")
        nc.vector.memset(zeros[:], 0.0)
        ident = keep.tile([P, P], F32, name="ident")
        make_identity(nc, ident[:])

        planes = [keep.tile([P, Q_OUT], U8, name="planes%d" % w, align_bytes=256) for w in range(4)]
        for w in range(4):
            nc.vector.memset(planes[w][:].bitcast(I32), 0)

        x_first = keep.tile([P, QUARTERS * 2 * K_PASS], BF16, name="x01", align_bytes=64)
        x_sb = [None, None] + [
            keep.tile([P, QUARTERS * K_PASS], BF16, name="x%d" % g, align_bytes=64) for g in range(2, GROUPS)
        ]
        w_sb = [
            [keep.tile([P, 4 * Q_OUT], U8, name="w%dg%d" % (w, g), align_bytes=256) for g in range(GROUPS)]
            for w in range(4)
        ]
        bias = keep.tile([P, Q_OUT], BF16, name="bias")
        x_by_group = x.rearrange("m (q g k) -> m q g k", q=QUARTERS, g=GROUPS)

        def load_first(pieces):
            count = QUARTERS // pieces
            dst = x_first[:].rearrange("p (q r) -> p q r", q=QUARTERS)
            src = x.rearrange("m (q r) -> m q r", q=QUARTERS)
            for piece in range(pieces):
                qs = slice(count * piece, count * (piece + 1))
                nc.sync.dma_start(out=dst[:, qs, :], in_=src[:, qs, 0 : 2 * K_PASS])

        def load_x(g, pieces=1):
            count = QUARTERS // pieces
            dst = x_sb[g][:].rearrange("p (q k) -> p q k", q=QUARTERS)
            for piece in range(pieces):
                qs = slice(count * piece, count * (piece + 1))
                nc.sync.dma_start(out=dst[:, qs, :], in_=x_by_group[:, qs, g, :])

        def load_scales(w):
            for quad in (0, 2, 1, 3):
                nc.sync.dma_start(
                    out=planes[w][32 * quad : 32 * quad + 16, :].bitcast(I32),
                    in_=scales_in[w][:, 4 * quad : 4 * quad + 4, :].bitcast(I32),
                )

        def load_words(w, g, pieces=1):
            width = 4 * Q_OUT // pieces
            source = words_in[w][g].rearrange("p n t -> p (n t)")
            for piece in range(pieces):
                cols = slice(width * piece, width * (piece + 1))
                nc.sync.dma_start(out=w_sb[w][g][:, cols].bitcast(I32), in_=source[:, cols].bitcast(I32))

        load_first(pieces=2)
        load_scales(0)
        load_words(0, 0, pieces=2)
        load_words(0, 1)
        load_scales(1)
        load_words(1, 0)
        load_words(1, 1)
        load_scales(2)
        load_words(2, 0)
        load_x(2)
        load_words(2, 1)
        load_words(0, 2)
        load_words(1, 2)
        load_x(3)
        load_words(2, 2)
        load_words(0, 3)
        load_words(1, 3)
        load_words(2, 3)
        load_scales(3)
        for g in range(GROUPS):
            load_words(3, g)
        nc.sync.dma_start(out=bias[:], in_=b.partition_broadcast(P))

        ordered = [None, None] + [
            keep.tile([P, QUARTERS * K_PASS // 2], F32, name="ord%d" % g, align_bytes=64) for g in range(2, GROUPS)
        ]
        grouped = [keep.tile([P, QUARTERS * K_PASS], BF16, name="grp%d" % g, align_bytes=64) for g in range(GROUPS)]
        negated = [keep.tile([P, QUARTERS * K_PASS], BF16, name="neg%d" % g, align_bytes=64) for g in range(GROUPS)]
        codes = {}
        xplanes = {}
        for q in range(QUARTERS):
            for sign in (1, -1):
                if q == 0 and sign == -1:
                    continue
                codes[(q, sign)] = keep.tile(
                    [P, SHIFT + Q_IN // 4], U32, name="xc%d_%d" % (q, sign + 1), align_bytes=256
                )
                xplanes[(q, sign)] = keep.tile([P, GROUPS, 256], U8, name="xs%d_%d" % (q, sign + 1), align_bytes=256)

        def quantise(q, sign, g):
            values = grouped[g] if sign == 1 else negated[g]
            nc.vector.quantize_mx(
                out=codes[(q, sign)][:, SHIFT + P * g : SHIFT + P * (g + 1)].bitcast(FP8X4),
                scales=xplanes[(q, sign)][:, g, 0:P],
                in_=values[:, K_PASS * q : K_PASS * (q + 1)],
            )

        def negate(g, q0, q1):
            cols = slice(K_PASS * q0, K_PASS * q1)
            nc.vector.tensor_scalar(
                out=negated[g][:, cols], in0=grouped[g][:, cols], scalar1=-1.0, scalar2=None, op0=MULT
            )

        def grouped_pair(g, pair):
            words = grouped[g][:].bitcast(F32).rearrange("p (q m u) -> p q m u", q=QUARTERS, u=2)
            return words[:, 2 * pair : 2 * pair + 2]

        warm = psum.tile([P, N_TILE], F32, name="warm", tag="bank3")

        def keep_clock_up(count):
            for i in range(count):
                nc.tensor.matmul(out=warm[:], lhsT=zeros[:, 0:P], rhs=zeros[:], start=True, stop=True)

        def prepare_first_two():
            x_words = x_first[:].bitcast(F32)
            banks = {}
            keep_clock_up(6)
            for pair in range(2):
                if pair == 1:
                    keep_clock_up(1)
                for g in range(2):
                    xt = psum.tile([P, 2, 2, P], F32, name="xt%d_%d" % (g, pair), tag="bank%d" % (6 - 2 * g + pair))
                    banks[(g, pair)] = xt[:].rearrange("p q u m -> p q m u")
                    for qq in range(2):
                        first = 512 * (2 * pair + qq) + 256 * g
                        for u in range(2):
                            nc.tensor.transpose(xt[:, qq, u, :], x_words[:, first + u : first + 256 : 2], ident[:])
            keep_clock_up(1)
            nc.scalar.copy(out=grouped_pair(0, 0), in_=banks[(0, 0)])
            nc.scalar.copy(out=grouped_pair(1, 0), in_=banks[(1, 0)])
            quantise(0, 1, 0)
            quantise(1, 1, 0)
            nc.vector.tensor_copy(out=grouped_pair(0, 1), in_=banks[(0, 1)])
            negate(0, 1, 2)
            quantise(2, 1, 0)
            quantise(3, 1, 0)
            nc.vector.tensor_copy(out=grouped_pair(1, 1), in_=banks[(1, 1)])
            quantise(0, 1, 1)
            quantise(1, 1, 1)
            quantise(2, 1, 1)
            quantise(3, 1, 1)
            negate(0, 2, 4)
            quantise(1, -1, 0)
            quantise(2, -1, 0)
            quantise(3, -1, 0)
            negate(1, 1, 4)
            quantise(1, -1, 1)
            quantise(2, -1, 1)
            quantise(3, -1, 1)

        def prepare_group(g):
            x_words = x_sb[g][:].bitcast(F32)
            grouped_words = grouped[g][:].bitcast(F32).rearrange("p (q m u) -> p q m u", q=QUARTERS, u=2)
            banks = []
            dst = ordered[g][:].rearrange("p (q u i) -> p q u i", q=QUARTERS, u=2)
            src = x_words.rearrange("p (q i u) -> p q u i", q=QUARTERS, u=2)
            nc.scalar.copy(out=dst[:, 0:2], in_=src[:, 0:2])
            nc.vector.tensor_copy(out=dst[:, 2:4], in_=src[:, 2:4])
            for pair in range(2):
                xt = psum.tile([P, 2, 2, P], F32, name="xt%d_%d" % (g, pair), tag="bank%d" % (6 + pair))
                banks.append(xt)
                for qq in range(2):
                    q = 2 * pair + qq
                    for u in range(2):
                        half = ordered[g][:, 256 * q + P * u : 256 * q + P * (u + 1)]
                        nc.tensor.transpose(xt[:, qq, u, :], half, ident[:])
            nc.scalar.copy(out=grouped_words[:, 0:2], in_=banks[0][:].rearrange("p q u m -> p q m u"))
            quantise(0, 1, g)
            quantise(1, 1, g)
            nc.vector.tensor_copy(out=grouped_words[:, 2:4], in_=banks[1][:].rearrange("p q u m -> p q m u"))
            negate(g, 1, 2)
            quantise(2, 1, g)
            quantise(3, 1, g)
            negate(g, 2, 4)
            quantise(1, -1, g)
            quantise(2, -1, g)
            quantise(3, -1, g)

        acc = {}

        def mx_pass(w, g, c, n0, width, bank, start, stop):
            key = SOURCE[w][c]
            nc.tensor.matmul_mx(
                out=acc[bank][:],
                lhsT=codes[key][:, SHIFT + P * g : SHIFT + P * (g + 1)].bitcast(FP8X4),
                lhsT_scale=xplanes[key][:, g, 0:P],
                rhs=w_sb[w][g][:, 4 * n0 : 4 * (n0 + width)].bitcast(FP8X4),
                rhs_scale=planes[w][4 * g : P, n0 : n0 + width],
                start=start,
                stop=stop,
            )

        def chunk(w, g):
            for c in range(3):
                for h in range(HALVES):
                    bank = 2 * c + h
                    if w == 0 and g == 0:
                        acc[bank] = psum.tile([P, N_TILE], F32, name="acc%d" % bank, tag="bank%d" % bank)
                    mx_pass(w, g, c, N_TILE * h, N_TILE, bank, w == 0 and g == 0, w == 3 and g == GROUPS - 1)

        def finish(bank, c, n0, width):
            result = keep.tile([P, width], F32, name="res%s" % bank)
            nc.vector.tensor_tensor(out=result[:], in0=acc[bank][:], in1=bias[:, n0 : n0 + width], op=ADD)
            nc.sync.dma_start(out=out[:, Q_OUT * c + n0 : Q_OUT * c + n0 + width], in_=result[:])

        prepare_first_two()
        chunk(0, 0)
        chunk(0, 1)
        chunk(1, 0)
        chunk(1, 1)
        chunk(2, 0)
        for g in range(2, GROUPS):
            prepare_group(g)
            chunk(2, g - 1)
            chunk(0, g)
            chunk(1, g)
        chunk(2, 3)
        for g in range(GROUPS):
            chunk(3, g)
        for c in range(3):
            for h in range(HALVES):
                finish(2 * c + h, c, N_TILE * h, N_TILE)
        for name, tag, n0, width in (("late0", 6, 0, 512), ("late1", 7, 512, 256), ("late2", 0, 768, 256)):
            acc[name] = psum.tile([P, width], F32, name=name, tag="bank%d" % tag)
            for w in range(4):
                for g in range(GROUPS):
                    mx_pass(w, g, 3, n0, width, name, w == 0 and g == 0, w == 3 and g == GROUPS - 1)
            finish(name, 3, n0, width)
